import numpy as np
import ml_dtypes


def mxq(x, axis, fmt="e4m3"):
    dtype, down = {"e4m3": (ml_dtypes.float8_e4m3fn, 7), "e5m2": (ml_dtypes.float8_e5m2, 14)}[fmt]
    v = np.moveaxis(np.asarray(x, np.float32).astype(ml_dtypes.bfloat16).astype(np.float64), axis, -1)
    blocks = v.reshape(v.shape[:-1] + (-1, 32))
    amax = np.abs(blocks).max(-1, keepdims=True)
    byte = np.maximum(np.where(amax > 0, np.frexp(amax)[1] - 1 + 127, 0) - down, 1)
    scale = np.exp2(byte - 127.0)
    codes = (blocks / scale).astype(np.float32).astype(dtype).astype(np.float64)
    return np.moveaxis((codes * scale).reshape(v.shape), -1, axis)


WIDE = False


def mx_kscale(k):
    if not WIDE:
        return np.ones(k)
    levels = np.array([10, -10, 5, -5, 0])
    if k % 512:
        return np.exp2(np.random.permutation(np.resize(levels, k // 32))).repeat(32)
    a = np.empty((k // 512, 16))
    for p in range(k // 512):
        a[p, :8] = np.random.permutation(np.resize(levels, 8))
        for g in range(8):
            far = levels[np.abs(levels - a[p, g]) >= 10]
            a[p, g + 8] = far[np.random.randint(len(far))]
    return np.exp2(a.ravel()).repeat(32)


BF16 = ml_dtypes.bfloat16


def bf(x):
    return np.asarray(x, np.float32).astype(BF16)


def f64(x):
    return np.asarray(x).astype(np.float64)


B, S, D, E, H = 8, 1024, 256, 512, 8
HD = E // H


def setup_inputs():
    s = mx_kscale(E)
    f = np.tile(s.reshape(H, HD), (S // H, 1))[:, None, :]
    return {"h_attn": bf(np.random.standard_normal((B, S, H, HD)) * np.sqrt(np.e / H) * f),
            "Wo": bf(np.random.standard_normal((E, D)) / np.sqrt(E) / s[:, None]),
            "bo": bf(np.random.standard_normal(D) * 0.1)}


def reference(h_attn, Wo, bo):
    merged = f64(h_attn).transpose(0, 2, 1, 3).reshape(B, S, E)
    return (mxq(merged, 2, "e4m3") @ mxq(f64(Wo), 0, "e4m3")) + f64(bo)

@@ -1,0 +1,179 @@
+import concourse.mybir as mybir
+from concourse.masks import make_identity
+
+BF16 = mybir.dt.bfloat16
+F32 = mybir.dt.float32
+U32 = mybir.dt.uint32
+U8 = mybir.dt.uint8
+FP8X4 = mybir.dt.float8_e4m3fn_x4
+
+P = 128
+B, S, H, HD = 8, 1024, 8, 64
+E = H * HD
+D = 256
+J = E // HD
+ROWS = S // J
+HALVES = 2
+PACK = 4
+PAIR = 2
+TWIN = 2
+UNIT_HEADS = 4
+UNITS_PER_BATCH = H // UNIT_HEADS
+UNITS = B * UNITS_PER_BATCH
+UNIT_PAIRS = UNIT_HEADS // PAIR
+HEADS_ON_VECTOR = 1
+FILL_UNITS = 2
+
+FLOPS = 2 * B * S * E * D
+
+
+def tile_multiheadrotaryattention_pb_t_kernel(tc, h_attn, Wo, bo, out):
+    nc = tc.nc
+    with tc.tile_pool(name="const", bufs=1) as const, tc.tile_pool(name="loads", bufs=B) as loads, tc.tile_pool(
+        name="work", bufs=4
+    ) as work, tc.tile_pool(name="results", bufs=UNITS) as results, tc.psum_pool(name="flipped", bufs=4) as flipped, tc.psum_pool(
+        name="sums", bufs=4
+    ) as sums, tc.manual_schedule():
+        x_raw = []
+        for b in range(B):
+            raw = loads.tile([P, J * H * HD], BF16, tag="raw")
+            x_raw.append(raw)
+        w_raw = const.tile([P, PACK, D], BF16)
+        bias_row = const.tile([P, D], BF16)
+        nc.vector.memset(bias_row[:], 0.0)
+        for b in range(B):
+            nc.sync.dma_start(out=x_raw[b][:], in_=h_attn[b].rearrange("(p j) h d -> p (j h d)", j=J))
+            if b == 0:
+                for f in range(2):
+                    for u in range(HALVES):
+                        nc.sync.dma_start(
+                            out=w_raw[64 * f : 64 * f + 64, 2 * u : 2 * u + 2, :].rearrange("p e c -> p (e c)"),
+                            in_=Wo.rearrange("(j f u i e) c -> f u j i (e c)", j=J, f=2, u=HALVES, e=2)[f, u],
+                        )
+                nc.sync.dma_start(out=bias_row[0:1, :], in_=bo.rearrange("(o c) -> o c", o=1))
+
+        identity = const.tile([P, P], F32)
+        make_identity(nc, identity[:])
+        even_odd = const.tile([P, P], F32)
+        nc.vector.tensor_copy(
+            out=even_odd[:].rearrange("p (a s) -> p a s", a=TWIN), in_=identity[:].rearrange("p (s a) -> p a s", a=TWIN)
+        )
+        ones = const.tile([P, P], BF16)
+        nc.vector.memset(ones[:], 1.0)
+
+        w_grouped = const.tile([P, D, PACK], BF16, align_bytes=64)
+        w_codes = const.tile([P, D], U32, align_bytes=64)
+        w_scales = const.tile([P, D], U8, align_bytes=64)
+        bias_pair = const.tile([P, PAIR, D], F32)
+
+        def prepare_weights_and_bias():
+            nc.vector.tensor_copy(out=w_grouped[:], in_=w_raw[:].rearrange("p t c -> p c t"))
+            bias_sum = sums.tile([P, PAIR, D], F32, tag="acc")
+            nc.tensor.matmul(out=bias_sum[:, 0, :], lhsT=ones[:], rhs=bias_row[:], start=True, stop=True)
+            for q in range(PAIR):
+                nc.vector.tensor_copy(out=bias_pair[:, q, :], in_=bias_sum[:, 0, :])
+            nc.vector.quantize_mx(
+                out=w_codes[:].bitcast(FP8X4), scales=w_scales[:], in_=w_grouped[:].rearrange("p c t -> p (c t)")
+            )
+
+        x_head, x_grouped, x_codes, x_scales, x_sums = {}, {}, {}, {}, {}
+
+        def reorder(unit):
+            b, part = divmod(unit, UNITS_PER_BATCH)
+            first = part * UNIT_HEADS
+            nv = UNIT_HEADS if unit < FILL_UNITS else HEADS_ON_VECTOR
+            by_head = work.tile([P, UNIT_HEADS * J * HD], BF16, tag="by_head")
+            nc.vector.tensor_copy(
+                out=by_head[:].rearrange("p (u g j w) -> p u g j w", u=HALVES, j=J, w=16)[:, :, 0 : 2 * nv],
+                in_=x_raw[b][:].rearrange("p (j g u w) -> p u g j w", j=J, u=HALVES, w=16)[
+                    :, :, 2 * first : 2 * (first + nv)
+                ],
+            )
+            if nv < UNIT_HEADS:
+                nc.scalar.copy(
+                    out=by_head[:]
+                    .bitcast(F32)
+                    .rearrange("p (u g j w) -> p u g j w", u=HALVES, j=J, w=8)[:, :, 2 * nv : 2 * UNIT_HEADS],
+                    in_=x_raw[b][:]
+                    .bitcast(F32)
+                    .rearrange("p (j g u w) -> p u g j w", j=J, u=HALVES, w=8)[
+                        :, :, 2 * (first + nv) : 2 * (first + UNIT_HEADS)
+                    ],
+                )
+            x_head[unit] = by_head
+
+        def transpose(unit):
+            words = x_head[unit][:].bitcast(F32)
+            grouped = work.tile([P, UNIT_HEADS * ROWS * PACK], BF16, tag="grouped", align_bytes=64)
+            grouped_words = grouped[:].bitcast(F32)
+            for pair in range(UNIT_PAIRS):
+                bank = flipped.tile([P, HALVES, TWIN, PAIR, ROWS // TWIN], F32, tag="bank")
+                for h in range(PAIR):
+                    for u in range(HALVES):
+                        first = (u * UNIT_HEADS + pair * PAIR + h) * P
+                        nc.tensor.transpose(
+                            bank[:, u, :, h, :],
+                            words[:, first : first + P],
+                            even_odd[:].rearrange("p (a s) -> p a s", a=TWIN),
+                        )
+                width = PAIR * ROWS * HALVES
+                nc.scalar.copy(
+                    out=grouped_words[:, pair * width : (pair + 1) * width].rearrange("p (c u) -> p c u", u=HALVES),
+                    in_=bank[:].rearrange("p u a h s -> p (a h s) u"),
+                )
+            x_grouped[unit] = grouped
+
+        def quantise(unit):
+            codes = work.tile([P, UNIT_HEADS * ROWS], U32, tag="codes", align_bytes=64)
+            scales = work.tile([P, UNIT_HEADS * ROWS], U8, tag="scales", align_bytes=64)
+            nc.vector.quantize_mx(out=codes[:].bitcast(FP8X4), scales=scales[:], in_=x_grouped[unit][:])
+            x_codes[unit] = codes
+            x_scales[unit] = scales
+
+        def multiply(unit):
+            x_sums[unit] = []
+            for pair in range(UNIT_PAIRS):
+                acc = sums.tile([P, PAIR, D], F32, tag="acc")
+                for q in range(PAIR):
+                    cols = slice((pair * PAIR + q) * ROWS, (pair * PAIR + q + 1) * ROWS)
+                    nc.tensor.matmul_mx(
+                        out=acc[:, q, :],
+                        lhsT=x_codes[unit][:, cols].bitcast(FP8X4),
+                        lhsT_scale=x_scales[unit][:, cols],
+                        rhs=w_codes[:].bitcast(FP8X4),
+                        rhs_scale=w_scales[:],
+                        start=True,
+                        stop=True,
+                    )
+                x_sums[unit].append(acc)
+
+        def add_bias_and_store(unit):
+            b, part = divmod(unit, UNITS_PER_BATCH)
+            result = results.tile([P, UNIT_HEADS, D], F32, tag="result")
+            for pair in range(UNIT_PAIRS):
+                nc.vector.tensor_tensor(
+                    out=result[:, pair * PAIR : (pair + 1) * PAIR, :],
+                    in0=x_sums[unit][pair][:],
+                    in1=bias_pair[:],
+                    op=mybir.AluOpType.add,
+                )
+            out_rows = out[b].rearrange("(g m a) c -> m g (a c)", m=P, a=TWIN)
+            nc.sync.dma_start(
+                out=out_rows[:, part * UNIT_PAIRS : (part + 1) * UNIT_PAIRS, :],
+                in_=result[:].rearrange("p (g a) c -> p g (a c)", a=TWIN),
+            )
+
+        reorder(0)
+        reorder(1)
+        prepare_weights_and_bias()
+        transpose(0)
+        for unit in range(UNITS):
+            if unit + 2 < UNITS:
+                reorder(unit + 2)
+            if unit + 1 < UNITS:
+                transpose(unit + 1)
+            quantise(unit)
+            multiply(unit)
+            if unit >= 1:
+                add_bias_and_store(unit - 1)
+        add_bias_and_store(UNITS - 1)

@@ -14,50 +14,64 @@ D = 256
 J = E // HD
 ROWS = S // J
 HALVES = 2
+RUN = 16
+BLOCKS = HD // (HALVES * RUN)
 PACK = 4
 PAIR = 2
-TWIN = 2
-UNIT_HEADS = 4
-UNITS_PER_BATCH = H // UNIT_HEADS
-UNITS = B * UNITS_PER_BATCH
-UNIT_PAIRS = UNIT_HEADS // PAIR
-HEADS_ON_VECTOR = 1
-FILL_UNITS = 2
+HEADS = 4
+PIECES = {0: 4, 1: 2}
+VECTOR_BLOCKS = 2
 
 FLOPS = 2 * B * S * E * D
 
 
 def tile_multiheadrotaryattention_pb_t_kernel(tc, h_attn, Wo, bo, out):
     nc = tc.nc
-    with tc.tile_pool(name="const", bufs=1) as const, tc.tile_pool(name="loads", bufs=B) as loads, tc.tile_pool(
-        name="work", bufs=4
-    ) as work, tc.tile_pool(name="results", bufs=UNITS) as results, tc.psum_pool(name="flipped", bufs=4) as flipped, tc.psum_pool(
+    units = [(b, h, HEADS) for b in range(B) for h in range(0, H, HEADS)]
+    last_b, last_h, last_n = units.pop()
+    units += [(last_b, h, PAIR) for h in range(last_h, last_h + last_n, PAIR)]
+    with tc.tile_pool(name="const", bufs=1) as const, tc.tile_pool(name="work", bufs=4) as work, tc.tile_pool(
+        name="results", bufs=1
+    ) as results, tc.psum_pool(name="flipped", bufs=4) as flipped, tc.psum_pool(
         name="sums", bufs=4
     ) as sums, tc.manual_schedule():
-        x_raw = []
-        for b in range(B):
-            raw = loads.tile([P, J * H * HD], BF16, tag="raw")
-            x_raw.append(raw)
         w_raw = const.tile([P, PACK, D], BF16)
         bias_row = const.tile([P, D], BF16)
         nc.vector.memset(bias_row[:], 0.0)
+        x_tokens = [h_attn[b].rearrange("(p j) h d -> p j (h d)", j=J) for b in range(B)]
+        x_raw = {}
         for b in range(B):
-            nc.sync.dma_start(out=x_raw[b][:], in_=h_attn[b].rearrange("(p j) h d -> p (j h d)", j=J))
-            if b == 0:
-                for f in range(2):
-                    for u in range(HALVES):
-                        nc.sync.dma_start(
-                            out=w_raw[64 * f : 64 * f + 64, 2 * u : 2 * u + 2, :].rearrange("p e c -> p (e c)"),
-                            in_=Wo.rearrange("(j f u i e) c -> f u j i (e c)", j=J, f=2, u=HALVES, e=2)[f, u],
-                        )
-                nc.sync.dma_start(out=bias_row[0:1, :], in_=bo.rearrange("(o c) -> o c", o=1))
+            pieces = PIECES.get(b, 1)
+            for c in range(pieces):
+                raw = const.tile([P, J // pieces, E], BF16, tag="raw%d_%d" % (b, c))
+                x_raw[b, c] = raw
+
+        def load(b, c):
+            tokens = J // PIECES.get(b, 1)
+            nc.sync.dma_start(out=x_raw[b, c][:], in_=x_tokens[b][:, c * tokens : (c + 1) * tokens, :])
+
+        load(0, 0)
+        nc.sync.dma_start(out=bias_row[0:1, :], in_=bo.rearrange("(o c) -> o c", o=1))
+        load(0, 1)
+        for f in range(BLOCKS):
+            for u in range(HALVES):
+                nc.sync.dma_start(
+                    out=w_raw[64 * f : 64 * f + 64, 2 * u : 2 * u + 2, :].rearrange("p e c -> p (e c)"),
+                    in_=Wo.rearrange("(j f u i e) c -> f u j i (e c)", j=J, f=BLOCKS, u=HALVES, e=2)[f, u],
+                )
+        load(0, 2)
+        load(0, 3)
+        for b in range(1, B):
+            for c in range(PIECES.get(b, 1)):
+                load(b, c)
 
         identity = const.tile([P, P], F32)
         make_identity(nc, identity[:])
-        even_odd = const.tile([P, P], F32)
-        nc.vector.tensor_copy(
-            out=even_odd[:].rearrange("p (a s) -> p a s", a=TWIN), in_=identity[:].rearrange("p (s a) -> p a s", a=TWIN)
-        )
+        spread = {}
+        for n in (HEADS, PAIR):
+            perm = const.tile([P, n, P // n], F32, tag="perm%d" % n)
+            nc.vector.tensor_copy(out=perm[:], in_=identity[:].rearrange("p (s a) -> p a s", a=n))
+            spread[n] = perm
         ones = const.tile([P, P], BF16)
         nc.vector.memset(ones[:], 1.0)
 
@@ -66,73 +80,71 @@ def tile_multiheadrotaryattention_pb_t_kernel(tc, h_attn, Wo, bo, out):
         w_scales = const.tile([P, D], U8, align_bytes=64)
         bias_pair = const.tile([P, PAIR, D], F32)
 
-        def prepare_weights_and_bias():
-            nc.vector.tensor_copy(out=w_grouped[:], in_=w_raw[:].rearrange("p t c -> p c t"))
-            bias_sum = sums.tile([P, PAIR, D], F32, tag="acc")
-            nc.tensor.matmul(out=bias_sum[:, 0, :], lhsT=ones[:], rhs=bias_row[:], start=True, stop=True)
-            for q in range(PAIR):
-                nc.vector.tensor_copy(out=bias_pair[:, q, :], in_=bias_sum[:, 0, :])
-            nc.vector.quantize_mx(
-                out=w_codes[:].bitcast(FP8X4), scales=w_scales[:], in_=w_grouped[:].rearrange("p c t -> p (c t)")
-            )
-
         x_head, x_grouped, x_codes, x_scales, x_sums = {}, {}, {}, {}, {}
 
-        def reorder(unit):
-            b, part = divmod(unit, UNITS_PER_BATCH)
-            first = part * UNIT_HEADS
-            nv = UNIT_HEADS if unit < FILL_UNITS else HEADS_ON_VECTOR
-            by_head = work.tile([P, UNIT_HEADS * J * HD], BF16, tag="by_head")
-            nc.vector.tensor_copy(
-                out=by_head[:].rearrange("p (u g j w) -> p u g j w", u=HALVES, j=J, w=16)[:, :, 0 : 2 * nv],
-                in_=x_raw[b][:].rearrange("p (j g u w) -> p u g j w", j=J, u=HALVES, w=16)[
-                    :, :, 2 * first : 2 * (first + nv)
-                ],
-            )
-            if nv < UNIT_HEADS:
-                nc.scalar.copy(
-                    out=by_head[:]
-                    .bitcast(F32)
-                    .rearrange("p (u g j w) -> p u g j w", u=HALVES, j=J, w=8)[:, :, 2 * nv : 2 * UNIT_HEADS],
-                    in_=x_raw[b][:]
-                    .bitcast(F32)
-                    .rearrange("p (j g u w) -> p u g j w", j=J, u=HALVES, w=8)[
-                        :, :, 2 * (first + nv) : 2 * (first + UNIT_HEADS)
-                    ],
-                )
+        def new_by_head(unit):
+            by_head = work.tile([P, HALVES * HEADS * BLOCKS * J * RUN], BF16, tag="by_head")
             x_head[unit] = by_head
 
+        def head_view(unit, dtype, run):
+            n = units[unit][2]
+            words = x_head[unit][:, 0 : n * E].bitcast(dtype) if dtype != BF16 else x_head[unit][:, 0 : n * E]
+            return words.rearrange("p (u g j w) -> p u g j w", u=HALVES, j=J, w=run)
+
+        def token_view(tokens, dtype, run):
+            flat = tokens[:].rearrange("p j e -> p (j e)")
+            flat = flat.bitcast(dtype) if dtype != BF16 else flat
+            return flat.rearrange("p (j g u w) -> p u g j w", g=H * BLOCKS, u=HALVES, w=run)
+
+        def reorder(unit, nv, c=0):
+            b, h, n = units[unit]
+            pieces = PIECES.get(b, 1)
+            tok = slice(c * J // pieces, (c + 1) * J // pieces)
+            g0, n = h * BLOCKS, n * BLOCKS
+            if c == 0:
+                new_by_head(unit)
+            if nv > 0:
+                nc.vector.tensor_copy(
+                    out=head_view(unit, BF16, RUN)[:, :, 0:nv, tok],
+                    in_=token_view(x_raw[b, c], BF16, RUN)[:, :, g0 : g0 + nv],
+                )
+            if nv < n:
+                nc.scalar.copy(
+                    out=head_view(unit, F32, RUN // 2)[:, :, nv:n, tok],
+                    in_=token_view(x_raw[b, c], F32, RUN // 2)[:, :, g0 + nv : g0 + n],
+                )
+
         def transpose(unit):
-            words = x_head[unit][:].bitcast(F32)
-            grouped = work.tile([P, UNIT_HEADS * ROWS * PACK], BF16, tag="grouped", align_bytes=64)
-            grouped_words = grouped[:].bitcast(F32)
-            for pair in range(UNIT_PAIRS):
-                bank = flipped.tile([P, HALVES, TWIN, PAIR, ROWS // TWIN], F32, tag="bank")
+            n = units[unit][2]
+            words = x_head[unit][:, 0 : n * E].bitcast(F32)
+            grouped = work.tile([P, HEADS * ROWS * PACK], BF16, tag="grouped", align_bytes=64)
+            grouped_words = grouped[:, 0 : n * E].bitcast(F32).rearrange("p (a c u) -> p a c u", a=n, u=HALVES)
+            cols = PAIR * ROWS // n
+            for pair in range(n // PAIR):
+                bank = flipped.tile([P, HALVES, n, PAIR, ROWS // n], F32, tag="bank")
                 for h in range(PAIR):
                     for u in range(HALVES):
-                        first = (u * UNIT_HEADS + pair * PAIR + h) * P
-                        nc.tensor.transpose(
-                            bank[:, u, :, h, :],
-                            words[:, first : first + P],
-                            even_odd[:].rearrange("p (a s) -> p a s", a=TWIN),
-                        )
-                width = PAIR * ROWS * HALVES
+                        first = (u * n + pair * PAIR + h) * P
+                        nc.tensor.transpose(bank[:, u, :, h, :], words[:, first : first + P], spread[n][:])
                 nc.scalar.copy(
-                    out=grouped_words[:, pair * width : (pair + 1) * width].rearrange("p (c u) -> p c u", u=HALVES),
-                    in_=bank[:].rearrange("p u a h s -> p (a h s) u"),
+                    out=grouped_words[:, :, pair * cols : (pair + 1) * cols, :],
+                    in_=bank[:].rearrange("p u a h s -> p a (h s) u"),
                 )
             x_grouped[unit] = grouped
 
         def quantise(unit):
-            codes = work.tile([P, UNIT_HEADS * ROWS], U32, tag="codes", align_bytes=64)
-            scales = work.tile([P, UNIT_HEADS * ROWS], U8, tag="scales", align_bytes=64)
-            nc.vector.quantize_mx(out=codes[:].bitcast(FP8X4), scales=scales[:], in_=x_grouped[unit][:])
+            n = units[unit][2]
+            codes = work.tile([P, HEADS * ROWS], U32, tag="codes", align_bytes=64)
+            scales = work.tile([P, HEADS * ROWS], U8, tag="scales", align_bytes=64)
+            nc.vector.quantize_mx(
+                out=codes[:, 0 : n * ROWS].bitcast(FP8X4), scales=scales[:, 0 : n * ROWS], in_=x_grouped[unit][:, 0 : n * E]
+            )
             x_codes[unit] = codes
             x_scales[unit] = scales
 
         def multiply(unit):
             x_sums[unit] = []
-            for pair in range(UNIT_PAIRS):
+            for pair in range(units[unit][2] // PAIR):
                 acc = sums.tile([P, PAIR, D], F32, tag="acc")
                 for q in range(PAIR):
                     cols = slice((pair * PAIR + q) * ROWS, (pair * PAIR + q + 1) * ROWS)
@@ -148,32 +160,56 @@ def tile_multiheadrotaryattention_pb_t_kernel(tc, h_attn, Wo, bo, out):
                 x_sums[unit].append(acc)
 
         def add_bias_and_store(unit):
-            b, part = divmod(unit, UNITS_PER_BATCH)
-            result = results.tile([P, UNIT_HEADS, D], F32, tag="result")
-            for pair in range(UNIT_PAIRS):
+            b, h, n = units[unit]
+            result = results.tile([P, n, D], F32, tag="result%d" % unit)
+            for pair in range(n // PAIR):
                 nc.vector.tensor_tensor(
                     out=result[:, pair * PAIR : (pair + 1) * PAIR, :],
                     in0=x_sums[unit][pair][:],
                     in1=bias_pair[:],
                     op=mybir.AluOpType.add,
                 )
-            out_rows = out[b].rearrange("(g m a) c -> m g (a c)", m=P, a=TWIN)
             nc.sync.dma_start(
-                out=out_rows[:, part * UNIT_PAIRS : (part + 1) * UNIT_PAIRS, :],
-                in_=result[:].rearrange("p (g a) c -> p g (a c)", a=TWIN),
+                out=out[b].rearrange("(g m a) c -> g m (a c)", m=P, a=n)[h // n],
+                in_=result[:].rearrange("p a c -> p (a c)"),
             )
 
-        reorder(0)
-        reorder(1)
-        prepare_weights_and_bias()
+        all_blocks = HEADS * BLOCKS
+        reorder(0, all_blocks, 0)
+        reorder(1, 0, 0)
+        bias_sum = sums.tile([P, PAIR, D], F32, tag="acc")
+        for q in range(PAIR):
+            nc.tensor.matmul(out=bias_sum[:, q, :], lhsT=ones[:], rhs=bias_row[:], start=True, stop=True)
+        nc.vector.tensor_copy(out=bias_pair[:], in_=bias_sum[:])
+        reorder(0, all_blocks, 1)
+        reorder(1, 0, 1)
+        nc.scalar.copy(out=w_grouped[:], in_=w_raw[:].rearrange("p t c -> p c t"))
+        reorder(0, all_blocks, 2)
+        reorder(1, 0, 2)
+        reorder(0, all_blocks, 3)
+        reorder(1, 0, 3)
         transpose(0)
-        for unit in range(UNITS):
-            if unit + 2 < UNITS:
-                reorder(unit + 2)
-            if unit + 1 < UNITS:
+        nc.vector.quantize_mx(
+            out=w_codes[:].bitcast(FP8X4), scales=w_scales[:], in_=w_grouped[:].rearrange("p c t -> p (c t)")
+        )
+        reorder(2, all_blocks, 0)
+        last = len(units) - 1
+        for unit in range(len(units)):
+            if unit == 0:
+                reorder(2, all_blocks, 1)
+            elif unit == 1:
+                reorder(3, VECTOR_BLOCKS, 0)
+                reorder(3, VECTOR_BLOCKS, 1)
+            elif unit + 2 < last:
+                reorder(unit + 2, VECTOR_BLOCKS * units[unit + 2][2] // HEADS)
+                if unit + 3 == last:
+                    reorder(last, VECTOR_BLOCKS * units[last][2] // HEADS)
+            if unit + 1 < last:
                 transpose(unit + 1)
+                if unit + 2 == last:
+                    transpose(last)
             quantise(unit)
             multiply(unit)
             if unit >= 1:
                 add_bias_and_store(unit - 1)
-        add_bias_and_store(UNITS - 1)
+        add_bias_and_store(last)

@@ -20,6 +20,7 @@ PACK = 4
 PAIR = 2
 HEADS = 4
 PIECES = {0: 4, 1: 2}
+EXTRA_PASSES = 2
 VECTOR_BLOCKS = 2
 
 FLOPS = 2 * B * S * E * D
@@ -146,6 +147,17 @@ def tile_multiheadrotaryattention_pb_t_kernel(tc, h_attn, Wo, bo, out):
             x_sums[unit] = []
             for pair in range(units[unit][2] // PAIR):
                 acc = sums.tile([P, PAIR, D], F32, tag="acc")
+                if pair == 0:
+                    for q in range(EXTRA_PASSES):
+                        nc.tensor.matmul_mx(
+                            out=acc[:, q % PAIR, :],
+                            lhsT=w_codes[:, 0:P].bitcast(FP8X4),
+                            lhsT_scale=w_scales[:, 0:P],
+                            rhs=w_codes[:].bitcast(FP8X4),
+                            rhs_scale=w_scales[:],
+                            start=True,
+                            stop=True,
+                        )
                 for q in range(PAIR):
                     cols = slice((pair * PAIR + q) * ROWS, (pair * PAIR + q + 1) * ROWS)
                     nc.tensor.matmul_mx(

@@ -206,22 +206,23 @@ def tile_multiheadrotaryattention_pb_t_kernel(tc, h_attn, Wo, bo, out):
         )
         reorder(2, all_blocks, 0)
         last = len(units) - 1
-        for unit in range(len(units)):
-            if unit == 0:
+        for step in range(last + 3):
+            if step == 0:
                 reorder(2, all_blocks, 1)
-            elif unit == 1:
+            elif step == 1:
                 reorder(3, VECTOR_BLOCKS, 0)
                 reorder(3, VECTOR_BLOCKS, 1)
-            elif unit + 2 < last:
-                reorder(unit + 2, VECTOR_BLOCKS * units[unit + 2][2] // HEADS)
-                if unit + 3 == last:
+            elif step + 2 < last:
+                reorder(step + 2, VECTOR_BLOCKS * units[step + 2][2] // HEADS)
+                if step + 3 == last:
                     reorder(last, VECTOR_BLOCKS * units[last][2] // HEADS)
-            if unit + 1 < last:
-                transpose(unit + 1)
-                if unit + 2 == last:
+            if step + 1 < last:
+                transpose(step + 1)
+                if step + 2 == last:
                     transpose(last)
-            quantise(unit)
-            multiply(unit)
-            if unit >= 1:
-                add_bias_and_store(unit - 1)
-        add_bias_and_store(last)
+            if step <= last:
+                quantise(step)
+            if 0 <= step - 1 <= last:
+                multiply(step - 1)
+            if step >= 2:
+                add_bias_and_store(step - 2)

@@ -19,9 +19,11 @@ BLOCKS = HD // (HALVES * RUN)
 PACK = 4
 PAIR = 2
 HEADS = 4
-PIECES = {0: 4, 1: 2}
+WHOLE = [(0, H, J)]
+PIECES = {0: [(0, HEADS, J // 2), (HEADS, HEADS, J)], 1: [(0, H, J // 2)]}
 EXTRA_PASSES = 2
 VECTOR_BLOCKS = 2
+FILL_BLOCKS = [5, 8, 8, 2]
 
 FLOPS = 2 * B * S * E * D
 
@@ -41,30 +43,27 @@ def tile_multiheadrotaryattention_pb_t_kernel(tc, h_attn, Wo, bo, out):
         nc.vector.memset(bias_row[:], 0.0)
         x_tokens = [h_attn[b].rearrange("(p j) h d -> p j (h d)", j=J) for b in range(B)]
         x_raw = {}
-        for b in range(B):
-            pieces = PIECES.get(b, 1)
-            for c in range(pieces):
-                raw = const.tile([P, J // pieces, E], BF16, tag="raw%d_%d" % (b, c))
-                x_raw[b, c] = raw
 
-        def load(b, c):
-            tokens = J // PIECES.get(b, 1)
-            nc.sync.dma_start(out=x_raw[b, c][:], in_=x_tokens[b][:, c * tokens : (c + 1) * tokens, :])
+        def load(b, first, heads, tokens):
+            for t in range(0, J, tokens):
+                raw = const.tile([P, tokens, heads * HD], BF16, tag="raw%d_%d_%d" % (b, first, t))
+                x_raw.setdefault((b, first), []).append(raw)
+                nc.sync.dma_start(
+                    out=raw[:], in_=x_tokens[b][:, t : t + tokens, first * HD : (first + heads) * HD]
+                )
 
-        load(0, 0)
+        load(0, *PIECES[0][0])
         nc.sync.dma_start(out=bias_row[0:1, :], in_=bo.rearrange("(o c) -> o c", o=1))
-        load(0, 1)
         for f in range(BLOCKS):
             for u in range(HALVES):
                 nc.sync.dma_start(
                     out=w_raw[64 * f : 64 * f + 64, 2 * u : 2 * u + 2, :].rearrange("p e c -> p (e c)"),
                     in_=Wo.rearrange("(j f u i e) c -> f u j i (e c)", j=J, f=BLOCKS, u=HALVES, e=2)[f, u],
                 )
-        load(0, 2)
-        load(0, 3)
+        load(0, *PIECES[0][1])
         for b in range(1, B):
-            for c in range(PIECES.get(b, 1)):
-                load(b, c)
+            for piece in PIECES.get(b, WHOLE):
+                load(b, *piece)
 
         identity = const.tile([P, P], F32)
         make_identity(nc, identity[:])
@@ -95,24 +94,27 @@ def tile_multiheadrotaryattention_pb_t_kernel(tc, h_attn, Wo, bo, out):
         def token_view(tokens, dtype, run):
             flat = tokens[:].rearrange("p j e -> p (j e)")
             flat = flat.bitcast(dtype) if dtype != BF16 else flat
-            return flat.rearrange("p (j g u w) -> p u g j w", g=H * BLOCKS, u=HALVES, w=run)
+            return flat.rearrange("p (j g u w) -> p u g j w", j=tokens.shape[1], u=HALVES, w=run)
 
-        def reorder(unit, nv, c=0):
+        def reorder(unit, c=0):
             b, h, n = units[unit]
-            pieces = PIECES.get(b, 1)
-            tok = slice(c * J // pieces, (c + 1) * J // pieces)
-            g0, n = h * BLOCKS, n * BLOCKS
+            blocks = FILL_BLOCKS[unit] if unit < len(FILL_BLOCKS) else VECTOR_BLOCKS
+            first = h if (b, h) in x_raw else 0
+            tokens = x_raw[b, first][c]
+            tok = slice(c * tokens.shape[1], (c + 1) * tokens.shape[1])
+            g0, n = (h - first) * BLOCKS, n * BLOCKS
+            nv = blocks * n // (HEADS * BLOCKS)
             if c == 0:
                 new_by_head(unit)
             if nv > 0:
                 nc.vector.tensor_copy(
                     out=head_view(unit, BF16, RUN)[:, :, 0:nv, tok],
-                    in_=token_view(x_raw[b, c], BF16, RUN)[:, :, g0 : g0 + nv],
+                    in_=token_view(tokens, BF16, RUN)[:, :, g0 : g0 + nv],
                 )
             if nv < n:
                 nc.scalar.copy(
                     out=head_view(unit, F32, RUN // 2)[:, :, nv:n, tok],
-                    in_=token_view(x_raw[b, c], F32, RUN // 2)[:, :, g0 + nv : g0 + n],
+                    in_=token_view(tokens, F32, RUN // 2)[:, :, g0 + nv : g0 + n],
                 )
 
         def transpose(unit):
@@ -186,43 +188,39 @@ def tile_multiheadrotaryattention_pb_t_kernel(tc, h_attn, Wo, bo, out):
                 in_=result[:].rearrange("p a c -> p (a c)"),
             )
 
-        all_blocks = HEADS * BLOCKS
-        reorder(0, all_blocks, 0)
-        reorder(1, 0, 0)
+        reorder(0, 0)
+        reorder(0, 1)
         bias_sum = sums.tile([P, PAIR, D], F32, tag="acc")
         for q in range(PAIR):
             nc.tensor.matmul(out=bias_sum[:, q, :], lhsT=ones[:], rhs=bias_row[:], start=True, stop=True)
-        nc.vector.tensor_copy(out=bias_pair[:], in_=bias_sum[:])
-        reorder(0, all_blocks, 1)
-        reorder(1, 0, 1)
-        nc.scalar.copy(out=w_grouped[:], in_=w_raw[:].rearrange("p t c -> p c t"))
-        reorder(0, all_blocks, 2)
-        reorder(1, 0, 2)
-        reorder(0, all_blocks, 3)
-        reorder(1, 0, 3)
-        transpose(0)
+        nc.scalar.copy(out=bias_pair[:], in_=bias_sum[:])
+        nc.vector.tensor_copy(out=w_grouped[:], in_=w_raw[:].rearrange("p t c -> p c t"))
         nc.vector.quantize_mx(
             out=w_codes[:].bitcast(FP8X4), scales=w_scales[:], in_=w_grouped[:].rearrange("p c t -> p (c t)")
         )
-        reorder(2, all_blocks, 0)
+        transpose(0)
+        reorder(1)
+        transpose(1)
+        quantise(0)
+        multiply(0)
+        reorder(2, 0)
+        reorder(2, 1)
         last = len(units) - 1
-        for step in range(last + 3):
-            if step == 0:
-                reorder(2, all_blocks, 1)
-            elif step == 1:
-                reorder(3, VECTOR_BLOCKS, 0)
-                reorder(3, VECTOR_BLOCKS, 1)
+        for step in range(1, last + 3):
+            if step == 1:
+                reorder(3, 0)
+                reorder(3, 1)
             elif step + 2 < last:
-                reorder(step + 2, VECTOR_BLOCKS * units[step + 2][2] // HEADS)
+                reorder(step + 2)
                 if step + 3 == last:
-                    reorder(last, VECTOR_BLOCKS * units[last][2] // HEADS)
+                    reorder(last)
             if step + 1 < last:
                 transpose(step + 1)
                 if step + 2 == last:
                     transpose(last)
-            if step <= last:
-                quantise(step)
-            if 0 <= step - 1 <= last:
+            if 2 <= step <= last + 1:
                 multiply(step - 1)
             if step >= 2:
                 add_bias_and_store(step - 2)
+            if step <= last:
+                quantise(step)

@@ -22,8 +22,10 @@ HEADS = 4
 WHOLE = [(0, H, J)]
 PIECES = {0: [(0, HEADS, J // 2), (HEADS, HEADS, J)], 1: [(0, H, J // 2)]}
 EXTRA_PASSES = 2
-VECTOR_BLOCKS = 2
-FILL_BLOCKS = [5, 8, 8, 2]
+VECTOR_BLOCKS = 1
+FILL_BLOCKS = [5, 8, 8]
+SLOTS = 4
+GROUPED_BYTES = HEADS * ROWS * PACK * 2
 
 FLOPS = 2 * B * S * E * D
 
@@ -35,7 +37,7 @@ def tile_multiheadrotaryattention_pb_t_kernel(tc, h_attn, Wo, bo, out):
     units += [(last_b, h, PAIR) for h in range(last_h, last_h + last_n, PAIR)]
     with tc.tile_pool(name="const", bufs=1) as const, tc.tile_pool(name="work", bufs=4) as work, tc.tile_pool(
         name="results", bufs=1
-    ) as results, tc.psum_pool(name="flipped", bufs=4) as flipped, tc.psum_pool(
+    ) as results, tc.tile_pool(name="turned", bufs=1) as turned, tc.psum_pool(name="flipped", bufs=4) as flipped, tc.psum_pool(
         name="sums", bufs=4
     ) as sums, tc.manual_schedule():
         w_raw = const.tile([P, PACK, D], BF16)
@@ -80,14 +82,20 @@ def tile_multiheadrotaryattention_pb_t_kernel(tc, h_attn, Wo, bo, out):
         w_scales = const.tile([P, D], U8, align_bytes=64)
         bias_pair = const.tile([P, PAIR, D], F32)
 
-        x_head, x_grouped, x_codes, x_scales, x_sums = {}, {}, {}, {}, {}
+        x_head, x_last, x_grouped, x_codes, x_scales, x_sums = {}, {}, {}, {}, {}, {}
+
+        def has_last(unit):
+            return len(FILL_BLOCKS) <= unit and units[unit][2] == HEADS
+
+        def own_heads(unit):
+            return units[unit][2] - (1 if has_last(unit) else 0)
 
         def new_by_head(unit):
             by_head = work.tile([P, HALVES * HEADS * BLOCKS * J * RUN], BF16, tag="by_head")
             x_head[unit] = by_head
 
         def head_view(unit, dtype, run):
-            n = units[unit][2]
+            n = own_heads(unit)
             words = x_head[unit][:, 0 : n * E].bitcast(dtype) if dtype != BF16 else x_head[unit][:, 0 : n * E]
             return words.rearrange("p (u g j w) -> p u g j w", u=HALVES, j=J, w=run)
 
@@ -102,10 +110,24 @@ def tile_multiheadrotaryattention_pb_t_kernel(tc, h_attn, Wo, bo, out):
             first = h if (b, h) in x_raw else 0
             tokens = x_raw[b, first][c]
             tok = slice(c * tokens.shape[1], (c + 1) * tokens.shape[1])
-            g0, n = (h - first) * BLOCKS, n * BLOCKS
-            nv = blocks * n // (HEADS * BLOCKS)
+            nv = blocks * n // HEADS
+            g0, n = (h - first) * BLOCKS, own_heads(unit) * BLOCKS
             if c == 0:
                 new_by_head(unit)
+            if has_last(unit):
+                if c == 0:
+                    slot = (unit + 1) % SLOTS
+                    last_head = turned.tile([P, E], BF16, tag="last%d" % slot, offset=slot * GROUPED_BYTES)
+                    x_last[unit] = last_head
+                for u in range(HALVES):
+                    nc.gpsimd.tensor_scalar(
+                        out=x_last[unit][:].rearrange("p (u g j w) -> p u g j w", u=HALVES, j=J, w=RUN)[:, u, :, tok],
+                        in0=token_view(tokens, BF16, RUN)[:, u, g0 + n : g0 + n + BLOCKS],
+                        scalar1=1.0,
+                        scalar2=0.0,
+                        op0=mybir.AluOpType.mult,
+                        op1=mybir.AluOpType.add,
+                    )
             if nv > 0:
                 nc.vector.tensor_copy(
                     out=head_view(unit, BF16, RUN)[:, :, 0:nv, tok],
@@ -119,16 +141,21 @@ def tile_multiheadrotaryattention_pb_t_kernel(tc, h_attn, Wo, bo, out):
 
         def transpose(unit):
             n = units[unit][2]
-            words = x_head[unit][:, 0 : n * E].bitcast(F32)
-            grouped = work.tile([P, HEADS * ROWS * PACK], BF16, tag="grouped", align_bytes=64)
+            own = own_heads(unit)
+            slot = unit % SLOTS
+            grouped = turned.tile([P, HEADS * ROWS * PACK], BF16, tag="grouped%d" % slot, offset=slot * GROUPED_BYTES)
             grouped_words = grouped[:, 0 : n * E].bitcast(F32).rearrange("p (a c u) -> p a c u", a=n, u=HALVES)
             cols = PAIR * ROWS // n
             for pair in range(n // PAIR):
                 bank = flipped.tile([P, HALVES, n, PAIR, ROWS // n], F32, tag="bank")
                 for h in range(PAIR):
                     for u in range(HALVES):
-                        first = (u * n + pair * PAIR + h) * P
-                        nc.tensor.transpose(bank[:, u, :, h, :], words[:, first : first + P], spread[n][:])
+                        head = pair * PAIR + h
+                        if head < own:
+                            words, first = x_head[unit][:, 0 : own * E], (u * own + head) * P
+                        else:
+                            words, first = x_last[unit][:], u * P
+                        nc.tensor.transpose(bank[:, u, :, h, :], words.bitcast(F32)[:, first : first + P], spread[n][:])
                 nc.scalar.copy(
                     out=grouped_words[:, :, pair * cols : (pair + 1) * cols, :],
                     in_=bank[:].rearrange("p u a h s -> p a (h s) u"),
@@ -206,7 +233,7 @@ def tile_multiheadrotaryattention_pb_t_kernel(tc, h_attn, Wo, bo, out):
         reorder(2, 0)
         reorder(2, 1)
         last = len(units) - 1
-        for step in range(1, last + 3):
+        for step in range(1, last + 2):
             if step == 1:
                 reorder(3, 0)
                 reorder(3, 1)
@@ -218,9 +245,8 @@ def tile_multiheadrotaryattention_pb_t_kernel(tc, h_attn, Wo, bo, out):
                 transpose(step + 1)
                 if step + 2 == last:
                     transpose(last)
-            if 2 <= step <= last + 1:
-                multiply(step - 1)
             if step >= 2:
-                add_bias_and_store(step - 2)
+                multiply(step - 1)
             if step <= last:
                 quantise(step)
+            add_bias_and_store(step - 1)

@@ -20,10 +20,10 @@ PACK = 4
 PAIR = 2
 HEADS = 4
 WHOLE = [(0, H, J)]
-PIECES = {0: [(0, HEADS, J // 2), (HEADS, HEADS, J)], 1: [(0, H, J // 2)]}
+PIECES = {0: [(0, H, J // 2)], 1: [(0, H, J // 2)]}
 EXTRA_PASSES = 2
 VECTOR_BLOCKS = 1
-FILL_BLOCKS = [5, 8, 8]
+FILL_BLOCKS = [5, 5, 8]
 SLOTS = 4
 GROUPED_BYTES = HEADS * ROWS * PACK * 2
 
@@ -62,7 +62,6 @@ def tile_multiheadrotaryattention_pb_t_kernel(tc, h_attn, Wo, bo, out):
                     out=w_raw[64 * f : 64 * f + 64, 2 * u : 2 * u + 2, :].rearrange("p e c -> p (e c)"),
                     in_=Wo.rearrange("(j f u i e) c -> f u j i (e c)", j=J, f=BLOCKS, u=HALVES, e=2)[f, u],
                 )
-        load(0, *PIECES[0][1])
         for b in range(1, B):
             for piece in PIECES.get(b, WHOLE):
                 load(b, *piece)
@@ -216,18 +215,19 @@ def tile_multiheadrotaryattention_pb_t_kernel(tc, h_attn, Wo, bo, out):
             )
 
         reorder(0, 0)
+        reorder(1, 0)
         reorder(0, 1)
+        reorder(1, 1)
+        transpose(0)
         bias_sum = sums.tile([P, PAIR, D], F32, tag="acc")
         for q in range(PAIR):
             nc.tensor.matmul(out=bias_sum[:, q, :], lhsT=ones[:], rhs=bias_row[:], start=True, stop=True)
+        transpose(1)
         nc.scalar.copy(out=bias_pair[:], in_=bias_sum[:])
         nc.vector.tensor_copy(out=w_grouped[:], in_=w_raw[:].rearrange("p t c -> p c t"))
         nc.vector.quantize_mx(
             out=w_codes[:].bitcast(FP8X4), scales=w_scales[:], in_=w_grouped[:].rearrange("p c t -> p (c t)")
         )
-        transpose(0)
-        reorder(1)
-        transpose(1)
         quantise(0)
         multiply(0)
         reorder(2, 0)

@@ -21,7 +21,7 @@ PAIR = 2
 HEADS = 4
 WHOLE = [(0, H, J)]
 PIECES = {0: [(0, H, J // 2)], 1: [(0, H, J // 2)]}
-EXTRA_PASSES = 2
+WARM_UP = 6
 VECTOR_BLOCKS = 1
 FILL_BLOCKS = [5, 5, 8]
 SLOTS = 4
@@ -43,6 +43,8 @@ def tile_multiheadrotaryattention_pb_t_kernel(tc, h_attn, Wo, bo, out):
         w_raw = const.tile([P, PACK, D], BF16)
         bias_row = const.tile([P, D], BF16)
         nc.vector.memset(bias_row[:], 0.0)
+        ones = const.tile([P, PAIR * D], BF16)
+        nc.vector.memset(ones[:], 1.0)
         x_tokens = [h_attn[b].rearrange("(p j) h d -> p j (h d)", j=J) for b in range(B)]
         x_raw = {}
 
@@ -73,8 +75,6 @@ def tile_multiheadrotaryattention_pb_t_kernel(tc, h_attn, Wo, bo, out):
             perm = const.tile([P, n, P // n], F32, tag="perm%d" % n)
             nc.vector.tensor_copy(out=perm[:], in_=identity[:].rearrange("p (s a) -> p a s", a=n))
             spread[n] = perm
-        ones = const.tile([P, P], BF16)
-        nc.vector.memset(ones[:], 1.0)
 
         w_grouped = const.tile([P, D, PACK], BF16, align_bytes=64)
         w_codes = const.tile([P, D], U32, align_bytes=64)
@@ -175,17 +175,6 @@ def tile_multiheadrotaryattention_pb_t_kernel(tc, h_attn, Wo, bo, out):
             x_sums[unit] = []
             for pair in range(units[unit][2] // PAIR):
                 acc = sums.tile([P, PAIR, D], F32, tag="acc")
-                if pair == 0:
-                    for q in range(EXTRA_PASSES):
-                        nc.tensor.matmul_mx(
-                            out=acc[:, q % PAIR, :],
-                            lhsT=w_codes[:, 0:P].bitcast(FP8X4),
-                            lhsT_scale=w_scales[:, 0:P],
-                            rhs=w_codes[:].bitcast(FP8X4),
-                            rhs_scale=w_scales[:],
-                            start=True,
-                            stop=True,
-                        )
                 for q in range(PAIR):
                     cols = slice((pair * PAIR + q) * ROWS, (pair * PAIR + q + 1) * ROWS)
                     nc.tensor.matmul_mx(
@@ -214,6 +203,11 @@ def tile_multiheadrotaryattention_pb_t_kernel(tc, h_attn, Wo, bo, out):
                 in_=result[:].rearrange("p a c -> p (a c)"),
             )
 
+        warm = sums.tile([P, PAIR, D], F32, tag="acc")
+        for q in range(WARM_UP):
+            nc.tensor.matmul(
+                out=warm[:].rearrange("p q c -> p (q c)"), lhsT=ones[:, 0:P], rhs=ones[:], start=True, stop=True
+            )
         reorder(0, 0)
         reorder(1, 0)
         reorder(0, 1)
@@ -221,7 +215,7 @@ def tile_multiheadrotaryattention_pb_t_kernel(tc, h_attn, Wo, bo, out):
         transpose(0)
         bias_sum = sums.tile([P, PAIR, D], F32, tag="acc")
         for q in range(PAIR):
-            nc.tensor.matmul(out=bias_sum[:, q, :], lhsT=ones[:], rhs=bias_row[:], start=True, stop=True)
+            nc.tensor.matmul(out=bias_sum[:, q, :], lhsT=ones[:, 0:P], rhs=bias_row[:], start=True, stop=True)
         transpose(1)
         nc.scalar.copy(out=bias_pair[:], in_=bias_sum[:])
         nc.vector.tensor_copy(out=w_grouped[:], in_=w_raw[:].rearrange("p t c -> p c t"))

@@ -22,8 +22,9 @@ HEADS = 4
 WHOLE = [(0, H, J)]
 PIECES = {0: [(0, H, J // 2)], 1: [(0, H, J // 2)]}
 WARM_UP = 6
-VECTOR_BLOCKS = 1
-FILL_BLOCKS = [5, 5, 8]
+VECTOR_HEADS = 1
+FILL_HEADS = [2, 2, 4]
+WHOLE_STORES = 5
 SLOTS = 4
 GROUPED_BYTES = HEADS * ROWS * PACK * 2
 
@@ -58,12 +59,11 @@ def tile_multiheadrotaryattention_pb_t_kernel(tc, h_attn, Wo, bo, out):
 
         load(0, *PIECES[0][0])
         nc.sync.dma_start(out=bias_row[0:1, :], in_=bo.rearrange("(o c) -> o c", o=1))
-        for f in range(BLOCKS):
-            for u in range(HALVES):
-                nc.sync.dma_start(
-                    out=w_raw[64 * f : 64 * f + 64, 2 * u : 2 * u + 2, :].rearrange("p e c -> p (e c)"),
-                    in_=Wo.rearrange("(j f u i e) c -> f u j i (e c)", j=J, f=BLOCKS, u=HALVES, e=2)[f, u],
-                )
+        for u in range(HALVES):
+            nc.sync.dma_start(
+                out=w_raw[:, 2 * u : 2 * u + 2, :].rearrange("p e c -> p (e c)"),
+                in_=Wo.rearrange("(k u i e) c -> u k i (e c)", k=J * BLOCKS, u=HALVES, e=2)[u],
+            )
         for b in range(1, B):
             for piece in PIECES.get(b, WHOLE):
                 load(b, *piece)
@@ -81,10 +81,10 @@ def tile_multiheadrotaryattention_pb_t_kernel(tc, h_attn, Wo, bo, out):
         w_scales = const.tile([P, D], U8, align_bytes=64)
         bias_pair = const.tile([P, PAIR, D], F32)
 
-        x_head, x_last, x_grouped, x_codes, x_scales, x_sums = {}, {}, {}, {}, {}, {}
+        x_head, x_last, x_grouped, x_codes, x_scales, x_sums, x_result = {}, {}, {}, {}, {}, {}, {}
 
         def has_last(unit):
-            return len(FILL_BLOCKS) <= unit and units[unit][2] == HEADS
+            return len(FILL_HEADS) <= unit and units[unit][2] == HEADS
 
         def own_heads(unit):
             return units[unit][2] - (1 if has_last(unit) else 0)
@@ -94,23 +94,29 @@ def tile_multiheadrotaryattention_pb_t_kernel(tc, h_attn, Wo, bo, out):
             x_head[unit] = by_head
 
         def head_view(unit, dtype, run):
-            n = own_heads(unit)
-            words = x_head[unit][:, 0 : n * E].bitcast(dtype) if dtype != BF16 else x_head[unit][:, 0 : n * E]
-            return words.rearrange("p (u g j w) -> p u g j w", u=HALVES, j=J, w=run)
+            words = x_head[unit][:, 0 : own_heads(unit) * E]
+            words = words.bitcast(dtype) if dtype != BF16 else words
+            return words.rearrange("p (u h j f w) -> p u h j f w", u=HALVES, j=J, f=BLOCKS, w=run)
 
         def token_view(tokens, dtype, run):
             flat = tokens[:].rearrange("p j e -> p (j e)")
             flat = flat.bitcast(dtype) if dtype != BF16 else flat
-            return flat.rearrange("p (j g u w) -> p u g j w", j=tokens.shape[1], u=HALVES, w=run)
+            return flat.rearrange("p (j h f u w) -> p u h j f w", j=tokens.shape[1], f=BLOCKS, u=HALVES, w=run)
+
+        def reorder_heads(copy, dst, src):
+            if dst.shape[2] == 1:
+                copy(out=dst[:, :, 0], in_=src[:, :, 0])
+            else:
+                for u in range(HALVES):
+                    copy(out=dst[:, u], in_=src[:, u])
 
         def reorder(unit, c=0):
             b, h, n = units[unit]
-            blocks = FILL_BLOCKS[unit] if unit < len(FILL_BLOCKS) else VECTOR_BLOCKS
-            first = h if (b, h) in x_raw else 0
-            tokens = x_raw[b, first][c]
+            heads = FILL_HEADS[unit] if unit < len(FILL_HEADS) else VECTOR_HEADS
+            tokens = x_raw[b, 0][c]
             tok = slice(c * tokens.shape[1], (c + 1) * tokens.shape[1])
-            nv = blocks * n // HEADS
-            g0, n = (h - first) * BLOCKS, own_heads(unit) * BLOCKS
+            own = own_heads(unit)
+            nv = heads if n == HEADS else 0
             if c == 0:
                 new_by_head(unit)
             if has_last(unit):
@@ -120,22 +126,24 @@ def tile_multiheadrotaryattention_pb_t_kernel(tc, h_attn, Wo, bo, out):
                     x_last[unit] = last_head
                 for u in range(HALVES):
                     nc.gpsimd.tensor_scalar(
-                        out=x_last[unit][:].rearrange("p (u g j w) -> p u g j w", u=HALVES, j=J, w=RUN)[:, u, :, tok],
-                        in0=token_view(tokens, BF16, RUN)[:, u, g0 + n : g0 + n + BLOCKS],
+                        out=x_last[unit][:].rearrange("p (u j f w) -> p u j f w", u=HALVES, j=J, w=RUN)[:, u, tok],
+                        in0=token_view(tokens, BF16, RUN)[:, u, h + own],
                         scalar1=1.0,
                         scalar2=0.0,
                         op0=mybir.AluOpType.mult,
                         op1=mybir.AluOpType.add,
                     )
             if nv > 0:
-                nc.vector.tensor_copy(
-                    out=head_view(unit, BF16, RUN)[:, :, 0:nv, tok],
-                    in_=token_view(tokens, BF16, RUN)[:, :, g0 : g0 + nv],
+                reorder_heads(
+                    nc.vector.tensor_copy,
+                    head_view(unit, BF16, RUN)[:, :, 0:nv, tok],
+                    token_view(tokens, BF16, RUN)[:, :, h : h + nv],
                 )
-            if nv < n:
-                nc.scalar.copy(
-                    out=head_view(unit, F32, RUN // 2)[:, :, nv:n, tok],
-                    in_=token_view(tokens, F32, RUN // 2)[:, :, g0 + nv : g0 + n],
+            if nv < own:
+                reorder_heads(
+                    nc.scalar.copy,
+                    head_view(unit, F32, RUN // 2)[:, :, nv:own, tok],
+                    token_view(tokens, F32, RUN // 2)[:, :, h + nv : h + own],
                 )
 
         def transpose(unit):
@@ -190,18 +198,24 @@ def tile_multiheadrotaryattention_pb_t_kernel(tc, h_attn, Wo, bo, out):
 
         def add_bias_and_store(unit):
             b, h, n = units[unit]
-            result = results.tile([P, n, D], F32, tag="result%d" % unit)
+            together = H // HEADS if b < WHOLE_STORES else 1
+            part = h // n % together
+            if part == 0:
+                result = results.tile([P, together, n, D], F32, tag="result%d" % unit)
+                x_result[b] = result
             for pair in range(n // PAIR):
                 nc.vector.tensor_tensor(
-                    out=result[:, pair * PAIR : (pair + 1) * PAIR, :],
+                    out=x_result[b][:, part, pair * PAIR : (pair + 1) * PAIR, :],
                     in0=x_sums[unit][pair][:],
                     in1=bias_pair[:],
                     op=mybir.AluOpType.add,
                 )
-            nc.sync.dma_start(
-                out=out[b].rearrange("(g m a) c -> g m (a c)", m=P, a=n)[h // n],
-                in_=result[:].rearrange("p a c -> p (a c)"),
-            )
+            if part == together - 1:
+                first = h // n - part
+                nc.sync.dma_start(
+                    out=out[b].rearrange("(g m a) c -> m g (a c)", m=P, a=n)[:, first : first + together, :],
+                    in_=x_result[b][:].rearrange("p g a c -> p g (a c)"),
+                )
 
         warm = sums.tile([P, PAIR, D], F32, tag="acc")
         for q in range(WARM_UP):

import concourse.mybir as mybir
from concourse.masks import make_identity

BF16 = mybir.dt.bfloat16
F32 = mybir.dt.float32
U32 = mybir.dt.uint32
U8 = mybir.dt.uint8
FP8X4 = mybir.dt.float8_e4m3fn_x4

P = 128
B, S, H, HD = 8, 1024, 8, 64
E = H * HD
D = 256
J = E // HD
ROWS = S // J
HALVES = 2
RUN = 16
BLOCKS = HD // (HALVES * RUN)
PACK = 4
PAIR = 2
HEADS = 4
WHOLE = [(0, H, J)]
PIECES = {0: [(0, H, J // 2)], 1: [(0, H, J // 2)]}
WARM_UP = 6
VECTOR_HEADS = 1
FILL_HEADS = [2, 2, 4]
WHOLE_STORES = 5
SLOTS = 4
GROUPED_BYTES = HEADS * ROWS * PACK * 2

FLOPS = 2 * B * S * E * D


def tile_multiheadrotaryattention_pb_t_kernel(tc, h_attn, Wo, bo, out):
    nc = tc.nc
    units = [(b, h, HEADS) for b in range(B) for h in range(0, H, HEADS)]
    last_b, last_h, last_n = units.pop()
    units += [(last_b, h, PAIR) for h in range(last_h, last_h + last_n, PAIR)]
    with tc.tile_pool(name="const", bufs=1) as const, tc.tile_pool(name="work", bufs=4) as work, tc.tile_pool(
        name="results", bufs=1
    ) as results, tc.tile_pool(name="turned", bufs=1) as turned, tc.psum_pool(name="flipped", bufs=4) as flipped, tc.psum_pool(
        name="sums", bufs=4
    ) as sums, tc.manual_schedule():
        w_raw = const.tile([P, PACK, D], BF16)
        bias_row = const.tile([P, D], BF16)
        nc.vector.memset(bias_row[:], 0.0)
        ones = const.tile([P, PAIR * D], BF16)
        nc.vector.memset(ones[:], 1.0)
        x_tokens = [h_attn[b].rearrange("(p j) h d -> p j (h d)", j=J) for b in range(B)]
        x_raw = {}

        def load(b, first, heads, tokens):
            for t in range(0, J, tokens):
                raw = const.tile([P, tokens, heads * HD], BF16, tag="raw%d_%d_%d" % (b, first, t))
                x_raw.setdefault((b, first), []).append(raw)
                nc.sync.dma_start(
                    out=raw[:], in_=x_tokens[b][:, t : t + tokens, first * HD : (first + heads) * HD]
                )

        load(0, *PIECES[0][0])
        nc.sync.dma_start(out=bias_row[0:1, :], in_=bo.rearrange("(o c) -> o c", o=1))
        for u in range(HALVES):
            nc.sync.dma_start(
                out=w_raw[:, 2 * u : 2 * u + 2, :].rearrange("p e c -> p (e c)"),
                in_=Wo.rearrange("(k u i e) c -> u k i (e c)", k=J * BLOCKS, u=HALVES, e=2)[u],
            )
        for b in range(1, B):
            for piece in PIECES.get(b, WHOLE):
                load(b, *piece)

        identity = const.tile([P, P], F32)
        make_identity(nc, identity[:])
        spread = {}
        for n in (HEADS, PAIR):
            perm = const.tile([P, n, P // n], F32, tag="perm%d" % n)
            nc.vector.tensor_copy(out=perm[:], in_=identity[:].rearrange("p (s a) -> p a s", a=n))
            spread[n] = perm

        w_grouped = const.tile([P, D, PACK], BF16, align_bytes=64)
        w_codes = const.tile([P, D], U32, align_bytes=64)
        w_scales = const.tile([P, D], U8, align_bytes=64)
        bias_pair = const.tile([P, PAIR, D], F32)

        x_head, x_last, x_grouped, x_codes, x_scales, x_sums, x_result = {}, {}, {}, {}, {}, {}, {}

        def has_last(unit):
            return len(FILL_HEADS) <= unit and units[unit][2] == HEADS

        def own_heads(unit):
            return units[unit][2] - (1 if has_last(unit) else 0)

        def new_by_head(unit):
            by_head = work.tile([P, HALVES * HEADS * BLOCKS * J * RUN], BF16, tag="by_head")
            x_head[unit] = by_head

        def head_view(unit, dtype, run):
            words = x_head[unit][:, 0 : own_heads(unit) * E]
            words = words.bitcast(dtype) if dtype != BF16 else words
            return words.rearrange("p (u h j f w) -> p u h j f w", u=HALVES, j=J, f=BLOCKS, w=run)

        def token_view(tokens, dtype, run):
            flat = tokens[:].rearrange("p j e -> p (j e)")
            flat = flat.bitcast(dtype) if dtype != BF16 else flat
            return flat.rearrange("p (j h f u w) -> p u h j f w", j=tokens.shape[1], f=BLOCKS, u=HALVES, w=run)

        def reorder_heads(copy, dst, src):
            if dst.shape[2] == 1:
                copy(out=dst[:, :, 0], in_=src[:, :, 0])
            else:
                for u in range(HALVES):
                    copy(out=dst[:, u], in_=src[:, u])

        def reorder(unit, c=0):
            b, h, n = units[unit]
            heads = FILL_HEADS[unit] if unit < len(FILL_HEADS) else VECTOR_HEADS
            tokens = x_raw[b, 0][c]
            tok = slice(c * tokens.shape[1], (c + 1) * tokens.shape[1])
            own = own_heads(unit)
            nv = heads if n == HEADS else 0
            if c == 0:
                new_by_head(unit)
            if has_last(unit):
                if c == 0:
                    slot = (unit + 1) % SLOTS
                    last_head = turned.tile([P, E], BF16, tag="last%d" % slot, offset=slot * GROUPED_BYTES)
                    x_last[unit] = last_head
                for u in range(HALVES):
                    nc.gpsimd.tensor_scalar(
                        out=x_last[unit][:].rearrange("p (u j f w) -> p u j f w", u=HALVES, j=J, w=RUN)[:, u, tok],
                        in0=token_view(tokens, BF16, RUN)[:, u, h + own],
                        scalar1=1.0,
                        scalar2=0.0,
                        op0=mybir.AluOpType.mult,
                        op1=mybir.AluOpType.add,
                    )
            if nv > 0:
                reorder_heads(
                    nc.vector.tensor_copy,
                    head_view(unit, BF16, RUN)[:, :, 0:nv, tok],
                    token_view(tokens, BF16, RUN)[:, :, h : h + nv],
                )
            if nv < own:
                reorder_heads(
                    nc.scalar.copy,
                    head_view(unit, F32, RUN // 2)[:, :, nv:own, tok],
                    token_view(tokens, F32, RUN // 2)[:, :, h + nv : h + own],
                )

        def transpose(unit):
            n = units[unit][2]
            own = own_heads(unit)
            slot = unit % SLOTS
            grouped = turned.tile([P, HEADS * ROWS * PACK], BF16, tag="grouped%d" % slot, offset=slot * GROUPED_BYTES)
            grouped_words = grouped[:, 0 : n * E].bitcast(F32).rearrange("p (a c u) -> p a c u", a=n, u=HALVES)
            cols = PAIR * ROWS // n
            for pair in range(n // PAIR):
                bank = flipped.tile([P, HALVES, n, PAIR, ROWS // n], F32, tag="bank")
                for h in range(PAIR):
                    for u in range(HALVES):
                        head = pair * PAIR + h
                        if head < own:
                            words, first = x_head[unit][:, 0 : own * E], (u * own + head) * P
                        else:
                            words, first = x_last[unit][:], u * P
                        nc.tensor.transpose(bank[:, u, :, h, :], words.bitcast(F32)[:, first : first + P], spread[n][:])
                nc.scalar.copy(
                    out=grouped_words[:, :, pair * cols : (pair + 1) * cols, :],
                    in_=bank[:].rearrange("p u a h s -> p a (h s) u"),
                )
            x_grouped[unit] = grouped

        def quantise(unit):
            n = units[unit][2]
            codes = work.tile([P, HEADS * ROWS], U32, tag="codes", align_bytes=64)
            scales = work.tile([P, HEADS * ROWS], U8, tag="scales", align_bytes=64)
            nc.vector.quantize_mx(
                out=codes[:, 0 : n * ROWS].bitcast(FP8X4), scales=scales[:, 0 : n * ROWS], in_=x_grouped[unit][:, 0 : n * E]
            )
            x_codes[unit] = codes
            x_scales[unit] = scales

        def multiply(unit):
            x_sums[unit] = []
            for pair in range(units[unit][2] // PAIR):
                acc = sums.tile([P, PAIR, D], F32, tag="acc")
                for q in range(PAIR):
                    cols = slice((pair * PAIR + q) * ROWS, (pair * PAIR + q + 1) * ROWS)
                    nc.tensor.matmul_mx(
                        out=acc[:, q, :],
                        lhsT=x_codes[unit][:, cols].bitcast(FP8X4),
                        lhsT_scale=x_scales[unit][:, cols],
                        rhs=w_codes[:].bitcast(FP8X4),
                        rhs_scale=w_scales[:],
                        start=True,
                        stop=True,
                    )
                x_sums[unit].append(acc)

        def add_bias_and_store(unit):
            b, h, n = units[unit]
            together = H // HEADS if b < WHOLE_STORES else 1
            part = h // n % together
            if part == 0:
                result = results.tile([P, together, n, D], F32, tag="result%d" % unit)
                x_result[b] = result
            for pair in range(n // PAIR):
                nc.vector.tensor_tensor(
                    out=x_result[b][:, part, pair * PAIR : (pair + 1) * PAIR, :],
                    in0=x_sums[unit][pair][:],
                    in1=bias_pair[:],
                    op=mybir.AluOpType.add,
                )
            if part == together - 1:
                first = h // n - part
                nc.sync.dma_start(
                    out=out[b].rearrange("(g m a) c -> m g (a c)", m=P, a=n)[:, first : first + together, :],
                    in_=x_result[b][:].rearrange("p g a c -> p g (a c)"),
                )

        warm = sums.tile([P, PAIR, D], F32, tag="acc")
        for q in range(WARM_UP):
            nc.tensor.matmul(
                out=warm[:].rearrange("p q c -> p (q c)"), lhsT=ones[:, 0:P], rhs=ones[:], start=True, stop=True
            )
        reorder(0, 0)
        reorder(1, 0)
        reorder(0, 1)
        reorder(1, 1)
        transpose(0)
        bias_sum = sums.tile([P, PAIR, D], F32, tag="acc")
        for q in range(PAIR):
            nc.tensor.matmul(out=bias_sum[:, q, :], lhsT=ones[:, 0:P], rhs=bias_row[:], start=True, stop=True)
        transpose(1)
        nc.scalar.copy(out=bias_pair[:], in_=bias_sum[:])
        nc.vector.tensor_copy(out=w_grouped[:], in_=w_raw[:].rearrange("p t c -> p c t"))
        nc.vector.quantize_mx(
            out=w_codes[:].bitcast(FP8X4), scales=w_scales[:], in_=w_grouped[:].rearrange("p c t -> p (c t)")
        )
        quantise(0)
        multiply(0)
        reorder(2, 0)
        reorder(2, 1)
        last = len(units) - 1
        for step in range(1, last + 2):
            if step == 1:
                reorder(3, 0)
                reorder(3, 1)
            elif step + 2 < last:
                reorder(step + 2)
                if step + 3 == last:
                    reorder(last)
            if step + 1 < last:
                transpose(step + 1)
                if step + 2 == last:
                    transpose(last)
            if step >= 2:
                multiply(step - 1)
            if step <= last:
                quantise(step)
            add_bias_and_store(step - 1)
